import numpy as np
import ml_dtypes


def mxq(x, axis, fmt="e4m3"):
    dtype, down = {"e4m3": (ml_dtypes.float8_e4m3fn, 7), "e5m2": (ml_dtypes.float8_e5m2, 14)}[fmt]
    v = np.moveaxis(np.asarray(x, np.float32).astype(ml_dtypes.bfloat16).astype(np.float64), axis, -1)
    blocks = v.reshape(v.shape[:-1] + (-1, 32))
    amax = np.abs(blocks).max(-1, keepdims=True)
    byte = np.maximum(np.where(amax > 0, np.frexp(amax)[1] - 1 + 127, 0) - down, 1)
    scale = np.exp2(byte - 127.0)
    codes = (blocks / scale).astype(np.float32).astype(dtype).astype(np.float64)
    return np.moveaxis((codes * scale).reshape(v.shape), -1, axis)


WIDE = False


def mx_kscale(k):
    if not WIDE:
        return np.ones(k)
    levels = np.array([10, -10, 5, -5, 0])
    a = np.random.permutation(np.resize(levels, k // 512 * 4)).reshape(k // 512, 4)
    idx = np.arange(k)
    return np.exp2(a[idx // 512, idx % 128 // 32])


BF16 = ml_dtypes.bfloat16


def bf(x):
    return np.asarray(x, np.float32).astype(BF16)


def f64(x):
    return np.asarray(x).astype(np.float64)


B, F, E, H, D0, D1 = 4096, 8, 128, 128, 64, 128
FH = F * H


def setup_inputs():
    t = mx_kscale(FH)
    tf = t.reshape(F, H)
    return {"x": bf(np.random.standard_normal((B, F, E))),
            "feat_w": bf(np.random.standard_normal((F, E, H)) / np.sqrt(E) * tf[:, None, :]),
            "feat_b": bf(np.random.standard_normal((F, H)) * 0.2 * tf),
            "trans_w": bf(np.random.standard_normal((FH, FH)) / np.sqrt(FH) / t[:, None] * t[None, :]),
            "trans_b": bf(np.random.standard_normal(FH) * 0.2 * t)}


def reference(x, feat_w, feat_b, trans_w, trans_b):
    pre = (f64(x).transpose(1, 0, 2) @ f64(feat_w)).transpose(1, 0, 2) + f64(feat_b)
    h = np.maximum(pre, 0.0)
    hf = h.reshape(B, FH)
    return np.maximum((mxq(hf, 1, "e4m3") @ mxq(f64(trans_w), 0, "e4m3")) + f64(trans_b), 0.0) + hf

@@ -1,0 +1,235 @@
+from contextlib import ExitStack
+
+import concourse.mybir as mybir
+from concourse.masks import make_identity
+
+BF16 = mybir.dt.bfloat16
+F32 = mybir.dt.float32
+U32 = mybir.dt.uint32
+U8 = mybir.dt.uint8
+FP8X4 = mybir.dt.float8_e4m3fn_x4
+ACT = mybir.ActivationFunctionType
+ALU = mybir.AluOpType
+
+P = 128
+BATCH = 4096
+FEATURES = 8
+HIDDEN = FEATURES * P
+PACK = 4
+PASSES = FEATURES // PACK
+
+CHUNK = 512
+ROWS = CHUNK // P
+CHUNKS = BATCH // CHUNK
+BANK = 512
+HALF = CHUNK // 2
+
+PARTS = 4
+LAG_LAYER = 1
+LAG_REGROUP = 3
+LAG_BIAS = 5
+LAG_MIX = 7
+LAG_FINISH = 8
+LAG_OUT = 12
+LOAD_AHEAD = 2
+
+FLOPS = 2 * BATCH * FEATURES * P * P + 2 * BATCH * HIDDEN * HIDDEN
+
+
+def tile_dsfs_pa_t_kernel(tc, x, feat_w, feat_b, trans_w, trans_b, out):
+    nc = tc.nc
+
+    x_chunks = x.rearrange("(i p r) f e -> i p r (f e)", p=P, r=ROWS)
+    out_chunks = out.rearrange("(i p r) n -> i p r n", p=P, r=ROWS)
+    w_passes = trans_w.rearrange("(g t p) n -> g p t n", t=PACK, p=P)
+
+    with ExitStack() as ctx:
+        ctx.enter_context(tc.manual_schedule())
+        const = ctx.enter_context(tc.tile_pool(name="const", bufs=1))
+        sbuf = ctx.enter_context(tc.tile_pool(name="sbuf", bufs=3))
+        psum = ctx.enter_context(tc.psum_pool(name="psum", bufs=2))
+
+        x_rows = {}
+        x_T = {}
+        h_T = {}
+        grouped = {}
+        h_codes = {}
+        h_scales = {}
+        sums = {}
+        out_rows = {}
+
+        def load_x(chunk):
+            x_rows[chunk] = sbuf.tile([P, ROWS, HIDDEN], BF16, name="x_rows", tag="x_rows")
+            nc.sync.dma_start(out=x_rows[chunk][:], in_=x_chunks[chunk])
+
+        feat_w_sb = const.tile([P, FEATURES, P], BF16)
+        nc.scalar.dma_start(out=feat_w_sb[:], in_=feat_w.rearrange("f e h -> e f h"))
+        bias_rows = const.tile([P, P], BF16)
+        nc.vector.memset(bias_rows[:], 0.0)
+        nc.scalar.dma_start(out=bias_rows[0:FEATURES, :], in_=feat_b)
+        nc.scalar.dma_start(
+            out=bias_rows[FEATURES : 2 * FEATURES, :],
+            in_=trans_b.rearrange("(f h) -> f h", f=FEATURES),
+        )
+        load_x(0)
+        w_raw = const.tile([P, PASSES, PACK, HIDDEN], BF16)
+        for g in range(PASSES):
+            nc.sync.dma_start(out=w_raw[:, g, :, :], in_=w_passes[g])
+        for chunk in range(1, LOAD_AHEAD):
+            load_x(chunk)
+
+        ident_bf16 = const.tile([P, P], BF16)
+        make_identity(nc, ident_bf16[:])
+        ident_f32 = const.tile([P, P], F32)
+        make_identity(nc, ident_f32[:])
+
+        bias_ps = psum.tile([P, P], BF16, tag="xT_ps")
+        nc.tensor.transpose(bias_ps[:], bias_rows[:], ident_bf16[:])
+        bias_cols = const.tile([P, 2 * FEATURES], F32)
+        nc.vector.tensor_copy(out=bias_cols[:], in_=bias_ps[:, 0 : 2 * FEATURES])
+        feat_b_col = bias_cols[:, 0:FEATURES]
+        trans_b_col = bias_cols[:, FEATURES : 2 * FEATURES]
+        neg_trans_b_col = const.tile([P, FEATURES], F32)
+        nc.vector.tensor_scalar(
+            out=neg_trans_b_col[:], in0=trans_b_col, scalar1=-1.0, scalar2=None, op0=ALU.mult
+        )
+
+        w_grouped = const.tile([P, PASSES, HIDDEN, PACK], BF16, align_bytes=64)
+        w_codes = const.tile([P, PASSES, HIDDEN], U32, align_bytes=64)
+        w_scales = const.tile([P, PASSES, HIDDEN], U8, align_bytes=64)
+        for g in range(PASSES):
+            nc.vector.tensor_copy(
+                out=w_grouped[:, g, :, :], in_=w_raw[:, g, :, :].rearrange("p t n -> p n t")
+            )
+        for g in range(PASSES):
+            nc.vector.quantize_mx(
+                out=w_codes[:, g, :].bitcast(FP8X4),
+                scales=w_scales[:, g, :],
+                in_=w_grouped[:, g, :, :].rearrange("p n t -> p (n t)"),
+            )
+
+        def transpose_x(chunk, part):
+            xT_ps = psum.tile([P, 2, CHUNK], BF16, tag="xT_ps")
+            for j in range(2):
+                f = 2 * part + j
+                for r in range(ROWS):
+                    nc.tensor.transpose(
+                        xT_ps[:, j, r * P : (r + 1) * P],
+                        x_rows[chunk][:, r, f * P : (f + 1) * P],
+                        ident_bf16[:],
+                    )
+            x_T[chunk, part] = sbuf.tile([P, 2, CHUNK], BF16, name="x_T", tag="x_T")
+            nc.scalar.copy(out=x_T[chunk, part][:], in_=xT_ps[:])
+
+        def feature_layers(chunk, part):
+            g = (2 * part) // PACK
+            if (2 * part) % PACK == 0:
+                h_T[chunk, g] = sbuf.tile([P, PACK, CHUNK], F32, name="h_T", tag="h_T", bufs=8)
+            for j in range(2):
+                f = 2 * part + j
+                pre_ps = psum.tile([P, CHUNK], F32, tag="pre_ps")
+                nc.tensor.matmul(
+                    pre_ps[:], lhsT=feat_w_sb[:, f, :], rhs=x_T[chunk, part][:, j, :],
+                    start=True, stop=True,
+                )
+                nc.scalar.activation(
+                    out=h_T[chunk, g][:, f % PACK, :], in_=pre_ps[:], func=ACT.Relu,
+                    bias=feat_b_col[:, f : f + 1], scale=1.0,
+                )
+
+        def regroup(chunk, part):
+            g, half = divmod(part, 2)
+            cols = slice(half * HALF, (half + 1) * HALF)
+            grouped[chunk, part] = sbuf.tile(
+                [P, HALF, PACK], BF16, name="grouped", tag="grouped", align_bytes=64
+            )
+            nc.vector.tensor_copy(
+                out=grouped[chunk, part][:],
+                in_=h_T[chunk, g][:, :, cols].rearrange("p t c -> p c t"),
+            )
+
+        def quantise(chunk, part):
+            g, half = divmod(part, 2)
+            cols = slice(half * HALF, (half + 1) * HALF)
+            if part == 0:
+                h_codes[chunk] = sbuf.tile(
+                    [P, PASSES, CHUNK], U32, name="h_codes", tag="h_codes", align_bytes=64
+                )
+                h_scales[chunk] = sbuf.tile(
+                    [P, PASSES, CHUNK], U8, name="h_scales", tag="h_scales", align_bytes=64
+                )
+            nc.vector.quantize_mx(
+                out=h_codes[chunk][:, g, cols].bitcast(FP8X4),
+                scales=h_scales[chunk][:, g, cols],
+                in_=grouped[chunk, part][:].rearrange("p c t -> p (c t)"),
+            )
+
+        def add_trans_b(chunk, part):
+            for n_tile in (2 * part, 2 * part + 1):
+                rows = h_T[chunk, n_tile // PACK][:, n_tile % PACK, :]
+                nc.vector.tensor_scalar(
+                    out=rows, in0=rows, scalar1=trans_b_col[:, n_tile : n_tile + 1],
+                    scalar2=None, op0=ALU.add,
+                )
+
+        def mix(chunk, part):
+            for n_tile in (2 * part, 2 * part + 1):
+                n_cols = slice(n_tile * P, (n_tile + 1) * P)
+                sums[chunk, n_tile] = psum.tile([P, CHUNK], F32, name="sums", tag="sums")
+                for g in range(PASSES):
+                    nc.tensor.matmul_mx(
+                        out=sums[chunk, n_tile][:],
+                        lhsT=w_codes[:, g, n_cols].bitcast(FP8X4),
+                        lhsT_scale=w_scales[:, g, n_cols],
+                        rhs=h_codes[chunk][:, g, :].bitcast(FP8X4),
+                        rhs_scale=h_scales[chunk][:, g, :],
+                        start=(g == 0),
+                        stop=(g == PASSES - 1),
+                    )
+
+        def finish(chunk, part):
+            for n_tile in (2 * part, 2 * part + 1):
+                rows = h_T[chunk, n_tile // PACK][:, n_tile % PACK, :]
+                nc.vector.scalar_tensor_tensor(
+                    out=rows, in0=sums[chunk, n_tile][:],
+                    scalar=neg_trans_b_col[:, n_tile : n_tile + 1], in1=rows,
+                    op0=ALU.max, op1=ALU.add,
+                )
+
+        def transpose_out(chunk, r):
+            if r % 2 == 0:
+                out_rows[chunk, r // 2] = sbuf.tile(
+                    [P, 2, HIDDEN], F32, name="out_rows", tag="out_rows"
+                )
+            for g in range(PASSES):
+                out_ps = psum.tile([P, BANK], F32, tag="out_ps")
+                for t in range(PACK):
+                    nc.tensor.transpose(
+                        out_ps[:, t * P : (t + 1) * P],
+                        h_T[chunk, g][:, t, r * P : (r + 1) * P],
+                        ident_f32[:],
+                    )
+                nc.scalar.copy(
+                    out=out_rows[chunk, r // 2][:, r % 2, g * BANK : (g + 1) * BANK], in_=out_ps[:]
+                )
+            if r % 2 == 1:
+                nc.sync.dma_start(
+                    out=out_chunks[chunk][:, r - 1 : r + 1, :], in_=out_rows[chunk, r // 2][:]
+                )
+
+        def run(stage, step, lag):
+            chunk, part = divmod(step - lag, PARTS)
+            if 0 <= chunk < CHUNKS:
+                stage(chunk, part)
+
+        for step in range(CHUNKS * PARTS + LAG_OUT):
+            if step % PARTS == 0 and step // PARTS + LOAD_AHEAD < CHUNKS:
+                load_x(step // PARTS + LOAD_AHEAD)
+            run(finish, step, LAG_FINISH)
+            run(transpose_out, step, LAG_OUT)
+            run(transpose_x, step, 0)
+            run(feature_layers, step, LAG_LAYER)
+            run(mix, step, LAG_MIX)
+            run(regroup, step, LAG_REGROUP)
+            run(add_trans_b, step, LAG_BIAS)
+            run(quantise, step, LAG_REGROUP)

@@ -23,6 +23,7 @@ ROWS = CHUNK // P
 CHUNKS = BATCH // CHUNK
 BANK = 512
 HALF = CHUNK // 2
+RUN = 4
 
 PARTS = 4
 LAG_LAYER = 1
@@ -56,22 +57,21 @@ def tile_dsfs_pa_t_kernel(tc, x, feat_w, feat_b, trans_w, trans_b, out):
         h_codes = {}
         h_scales = {}
         sums = {}
-        out_rows = {}
 
         def load_x(chunk):
             x_rows[chunk] = sbuf.tile([P, ROWS, HIDDEN], BF16, name="x_rows", tag="x_rows")
             nc.sync.dma_start(out=x_rows[chunk][:], in_=x_chunks[chunk])
 
-        feat_w_sb = const.tile([P, FEATURES, P], BF16)
-        nc.scalar.dma_start(out=feat_w_sb[:], in_=feat_w.rearrange("f e h -> e f h"))
         bias_rows = const.tile([P, P], BF16)
         nc.vector.memset(bias_rows[:], 0.0)
-        nc.scalar.dma_start(out=bias_rows[0:FEATURES, :], in_=feat_b)
-        nc.scalar.dma_start(
+        nc.sync.dma_start(out=bias_rows[0:FEATURES, :], in_=feat_b)
+        nc.sync.dma_start(
             out=bias_rows[FEATURES : 2 * FEATURES, :],
             in_=trans_b.rearrange("(f h) -> f h", f=FEATURES),
         )
         load_x(0)
+        feat_w_sb = const.tile([P, FEATURES, P], BF16)
+        nc.sync.dma_start(out=feat_w_sb[:], in_=feat_w.rearrange("f e h -> e f h"))
         w_raw = const.tile([P, PASSES, PACK, HIDDEN], BF16)
         for g in range(PASSES):
             nc.sync.dma_start(out=w_raw[:, g, :, :], in_=w_passes[g])
@@ -99,7 +99,8 @@ def tile_dsfs_pa_t_kernel(tc, x, feat_w, feat_b, trans_w, trans_b, out):
         w_scales = const.tile([P, PASSES, HIDDEN], U8, align_bytes=64)
         for g in range(PASSES):
             nc.vector.tensor_copy(
-                out=w_grouped[:, g, :, :], in_=w_raw[:, g, :, :].rearrange("p t n -> p n t")
+                out=w_grouped[:, g, :, :].rearrange("p (c i) t -> p c t i", i=RUN),
+                in_=w_raw[:, g, :, :].rearrange("p t (c i) -> p c t i", i=RUN),
             )
         for g in range(PASSES):
             nc.vector.quantize_mx(
@@ -144,8 +145,8 @@ def tile_dsfs_pa_t_kernel(tc, x, feat_w, feat_b, trans_w, trans_b, out):
                 [P, HALF, PACK], BF16, name="grouped", tag="grouped", align_bytes=64
             )
             nc.vector.tensor_copy(
-                out=grouped[chunk, part][:],
-                in_=h_T[chunk, g][:, :, cols].rearrange("p t c -> p c t"),
+                out=grouped[chunk, part][:].rearrange("p (c i) t -> p c t i", i=RUN),
+                in_=h_T[chunk, g][:, :, cols].rearrange("p t (c i) -> p c t i", i=RUN),
             )
 
         def quantise(chunk, part):
@@ -197,10 +198,7 @@ def tile_dsfs_pa_t_kernel(tc, x, feat_w, feat_b, trans_w, trans_b, out):
                 )
 
         def transpose_out(chunk, r):
-            if r % 2 == 0:
-                out_rows[chunk, r // 2] = sbuf.tile(
-                    [P, 2, HIDDEN], F32, name="out_rows", tag="out_rows"
-                )
+            out_rows = sbuf.tile([P, HIDDEN], F32, tag="out_rows", bufs=4)
             for g in range(PASSES):
                 out_ps = psum.tile([P, BANK], F32, tag="out_ps")
                 for t in range(PACK):
@@ -209,13 +207,8 @@ def tile_dsfs_pa_t_kernel(tc, x, feat_w, feat_b, trans_w, trans_b, out):
                         h_T[chunk, g][:, t, r * P : (r + 1) * P],
                         ident_f32[:],
                     )
-                nc.scalar.copy(
-                    out=out_rows[chunk, r // 2][:, r % 2, g * BANK : (g + 1) * BANK], in_=out_ps[:]
-                )
-            if r % 2 == 1:
-                nc.sync.dma_start(
-                    out=out_chunks[chunk][:, r - 1 : r + 1, :], in_=out_rows[chunk, r // 2][:]
-                )
+                nc.scalar.copy(out=out_rows[:, g * BANK : (g + 1) * BANK], in_=out_ps[:])
+            nc.sync.dma_start(out=out_chunks[chunk][:, r, :], in_=out_rows[:])
 
         def run(stage, step, lag):
             chunk, part = divmod(step - lag, PARTS)

@@ -28,6 +28,7 @@ RUN = 4
 PARTS = 4
 LAG_LAYER = 1
 LAG_REGROUP = 3
+LAG_QUANTISE = 4
 LAG_BIAS = 5
 LAG_MIX = 7
 LAG_FINISH = 8
@@ -168,9 +169,9 @@ def tile_dsfs_pa_t_kernel(tc, x, feat_w, feat_b, trans_w, trans_b, out):
         def add_trans_b(chunk, part):
             for n_tile in (2 * part, 2 * part + 1):
                 rows = h_T[chunk, n_tile // PACK][:, n_tile % PACK, :]
-                nc.vector.tensor_scalar(
-                    out=rows, in0=rows, scalar1=trans_b_col[:, n_tile : n_tile + 1],
-                    scalar2=None, op0=ALU.add,
+                nc.gpsimd.tensor_scalar(
+                    out=rows, in0=rows, scalar1=1.0, scalar2=trans_b_col[:, n_tile : n_tile + 1],
+                    op0=ALU.mult, op1=ALU.add,
                 )
 
         def mix(chunk, part):
@@ -207,7 +208,10 @@ def tile_dsfs_pa_t_kernel(tc, x, feat_w, feat_b, trans_w, trans_b, out):
                         h_T[chunk, g][:, t, r * P : (r + 1) * P],
                         ident_f32[:],
                     )
-                nc.scalar.copy(out=out_rows[:, g * BANK : (g + 1) * BANK], in_=out_ps[:])
+                if g == 0:
+                    nc.scalar.copy(out=out_rows[:, g * BANK : (g + 1) * BANK], in_=out_ps[:])
+                else:
+                    nc.vector.tensor_copy(out=out_rows[:, g * BANK : (g + 1) * BANK], in_=out_ps[:])
             nc.sync.dma_start(out=out_chunks[chunk][:, r, :], in_=out_rows[:])
 
         def run(stage, step, lag):
@@ -218,6 +222,7 @@ def tile_dsfs_pa_t_kernel(tc, x, feat_w, feat_b, trans_w, trans_b, out):
         for step in range(CHUNKS * PARTS + LAG_OUT):
             if step % PARTS == 0 and step // PARTS + LOAD_AHEAD < CHUNKS:
                 load_x(step // PARTS + LOAD_AHEAD)
+            run(quantise, step, LAG_QUANTISE)
             run(finish, step, LAG_FINISH)
             run(transpose_out, step, LAG_OUT)
             run(transpose_x, step, 0)
@@ -225,4 +230,3 @@ def tile_dsfs_pa_t_kernel(tc, x, feat_w, feat_b, trans_w, trans_b, out):
             run(mix, step, LAG_MIX)
             run(regroup, step, LAG_REGROUP)
             run(add_trans_b, step, LAG_BIAS)
-            run(quantise, step, LAG_REGROUP)

from contextlib import ExitStack

import concourse.mybir as mybir
from concourse.masks import make_identity

BF16 = mybir.dt.bfloat16
F32 = mybir.dt.float32
U32 = mybir.dt.uint32
U8 = mybir.dt.uint8
FP8X4 = mybir.dt.float8_e4m3fn_x4
ACT = mybir.ActivationFunctionType
ALU = mybir.AluOpType

P = 128
BATCH = 4096
FEATURES = 8
HIDDEN = FEATURES * P
PACK = 4
PASSES = FEATURES // PACK

CHUNK = 512
ROWS = CHUNK // P
CHUNKS = BATCH // CHUNK
BANK = 512
HALF = CHUNK // 2
RUN = 4

PARTS = 4
LAG_LAYER = 1
LAG_REGROUP = 3
LAG_QUANTISE = 4
LAG_BIAS = 5
LAG_MIX = 7
LAG_FINISH = 8
LAG_OUT = 12
LOAD_AHEAD = 2

FLOPS = 2 * BATCH * FEATURES * P * P + 2 * BATCH * HIDDEN * HIDDEN


def tile_dsfs_pa_t_kernel(tc, x, feat_w, feat_b, trans_w, trans_b, out):
    nc = tc.nc

    x_chunks = x.rearrange("(i p r) f e -> i p r (f e)", p=P, r=ROWS)
    out_chunks = out.rearrange("(i p r) n -> i p r n", p=P, r=ROWS)
    w_passes = trans_w.rearrange("(g t p) n -> g p t n", t=PACK, p=P)

    with ExitStack() as ctx:
        ctx.enter_context(tc.manual_schedule())
        const = ctx.enter_context(tc.tile_pool(name="const", bufs=1))
        sbuf = ctx.enter_context(tc.tile_pool(name="sbuf", bufs=3))
        psum = ctx.enter_context(tc.psum_pool(name="psum", bufs=2))

        x_rows = {}
        x_T = {}
        h_T = {}
        grouped = {}
        h_codes = {}
        h_scales = {}
        sums = {}

        def load_x(chunk):
            x_rows[chunk] = sbuf.tile([P, ROWS, HIDDEN], BF16, name="x_rows", tag="x_rows")
            nc.sync.dma_start(out=x_rows[chunk][:], in_=x_chunks[chunk])

        bias_rows = const.tile([P, P], BF16)
        nc.vector.memset(bias_rows[:], 0.0)
        nc.sync.dma_start(out=bias_rows[0:FEATURES, :], in_=feat_b)
        nc.sync.dma_start(
            out=bias_rows[FEATURES : 2 * FEATURES, :],
            in_=trans_b.rearrange("(f h) -> f h", f=FEATURES),
        )
        load_x(0)
        feat_w_sb = const.tile([P, FEATURES, P], BF16)
        nc.sync.dma_start(out=feat_w_sb[:], in_=feat_w.rearrange("f e h -> e f h"))
        w_raw = const.tile([P, PASSES, PACK, HIDDEN], BF16)
        for g in range(PASSES):
            nc.sync.dma_start(out=w_raw[:, g, :, :], in_=w_passes[g])
        for chunk in range(1, LOAD_AHEAD):
            load_x(chunk)

        ident_bf16 = const.tile([P, P], BF16)
        make_identity(nc, ident_bf16[:])
        ident_f32 = const.tile([P, P], F32)
        make_identity(nc, ident_f32[:])

        bias_ps = psum.tile([P, P], BF16, tag="xT_ps")
        nc.tensor.transpose(bias_ps[:], bias_rows[:], ident_bf16[:])
        bias_cols = const.tile([P, 2 * FEATURES], F32)
        nc.vector.tensor_copy(out=bias_cols[:], in_=bias_ps[:, 0 : 2 * FEATURES])
        feat_b_col = bias_cols[:, 0:FEATURES]
        trans_b_col = bias_cols[:, FEATURES : 2 * FEATURES]
        neg_trans_b_col = const.tile([P, FEATURES], F32)
        nc.vector.tensor_scalar(
            out=neg_trans_b_col[:], in0=trans_b_col, scalar1=-1.0, scalar2=None, op0=ALU.mult
        )

        w_grouped = const.tile([P, PASSES, HIDDEN, PACK], BF16, align_bytes=64)
        w_codes = const.tile([P, PASSES, HIDDEN], U32, align_bytes=64)
        w_scales = const.tile([P, PASSES, HIDDEN], U8, align_bytes=64)
        for g in range(PASSES):
            nc.vector.tensor_copy(
                out=w_grouped[:, g, :, :].rearrange("p (c i) t -> p c t i", i=RUN),
                in_=w_raw[:, g, :, :].rearrange("p t (c i) -> p c t i", i=RUN),
            )
        for g in range(PASSES):
            nc.vector.quantize_mx(
                out=w_codes[:, g, :].bitcast(FP8X4),
                scales=w_scales[:, g, :],
                in_=w_grouped[:, g, :, :].rearrange("p n t -> p (n t)"),
            )

        def transpose_x(chunk, part):
            xT_ps = psum.tile([P, 2, CHUNK], BF16, tag="xT_ps")
            for j in range(2):
                f = 2 * part + j
                for r in range(ROWS):
                    nc.tensor.transpose(
                        xT_ps[:, j, r * P : (r + 1) * P],
                        x_rows[chunk][:, r, f * P : (f + 1) * P],
                        ident_bf16[:],
                    )
            x_T[chunk, part] = sbuf.tile([P, 2, CHUNK], BF16, name="x_T", tag="x_T")
            nc.scalar.copy(out=x_T[chunk, part][:], in_=xT_ps[:])

        def feature_layers(chunk, part):
            g = (2 * part) // PACK
            if (2 * part) % PACK == 0:
                h_T[chunk, g] = sbuf.tile([P, PACK, CHUNK], F32, name="h_T", tag="h_T", bufs=8)
            for j in range(2):
                f = 2 * part + j
                pre_ps = psum.tile([P, CHUNK], F32, tag="pre_ps")
                nc.tensor.matmul(
                    pre_ps[:], lhsT=feat_w_sb[:, f, :], rhs=x_T[chunk, part][:, j, :],
                    start=True, stop=True,
                )
                nc.scalar.activation(
                    out=h_T[chunk, g][:, f % PACK, :], in_=pre_ps[:], func=ACT.Relu,
                    bias=feat_b_col[:, f : f + 1], scale=1.0,
                )

        def regroup(chunk, part):
            g, half = divmod(part, 2)
            cols = slice(half * HALF, (half + 1) * HALF)
            grouped[chunk, part] = sbuf.tile(
                [P, HALF, PACK], BF16, name="grouped", tag="grouped", align_bytes=64
            )
            nc.vector.tensor_copy(
                out=grouped[chunk, part][:].rearrange("p (c i) t -> p c t i", i=RUN),
                in_=h_T[chunk, g][:, :, cols].rearrange("p t (c i) -> p c t i", i=RUN),
            )

        def quantise(chunk, part):
            g, half = divmod(part, 2)
            cols = slice(half * HALF, (half + 1) * HALF)
            if part == 0:
                h_codes[chunk] = sbuf.tile(
                    [P, PASSES, CHUNK], U32, name="h_codes", tag="h_codes", align_bytes=64
                )
                h_scales[chunk] = sbuf.tile(
                    [P, PASSES, CHUNK], U8, name="h_scales", tag="h_scales", align_bytes=64
                )
            nc.vector.quantize_mx(
                out=h_codes[chunk][:, g, cols].bitcast(FP8X4),
                scales=h_scales[chunk][:, g, cols],
                in_=grouped[chunk, part][:].rearrange("p c t -> p (c t)"),
            )

        def add_trans_b(chunk, part):
            for n_tile in (2 * part, 2 * part + 1):
                rows = h_T[chunk, n_tile // PACK][:, n_tile % PACK, :]
                nc.gpsimd.tensor_scalar(
                    out=rows, in0=rows, scalar1=1.0, scalar2=trans_b_col[:, n_tile : n_tile + 1],
                    op0=ALU.mult, op1=ALU.add,
                )

        def mix(chunk, part):
            for n_tile in (2 * part, 2 * part + 1):
                n_cols = slice(n_tile * P, (n_tile + 1) * P)
                sums[chunk, n_tile] = psum.tile([P, CHUNK], F32, name="sums", tag="sums")
                for g in range(PASSES):
                    nc.tensor.matmul_mx(
                        out=sums[chunk, n_tile][:],
                        lhsT=w_codes[:, g, n_cols].bitcast(FP8X4),
                        lhsT_scale=w_scales[:, g, n_cols],
                        rhs=h_codes[chunk][:, g, :].bitcast(FP8X4),
                        rhs_scale=h_scales[chunk][:, g, :],
                        start=(g == 0),
                        stop=(g == PASSES - 1),
                    )

        def finish(chunk, part):
            for n_tile in (2 * part, 2 * part + 1):
                rows = h_T[chunk, n_tile // PACK][:, n_tile % PACK, :]
                nc.vector.scalar_tensor_tensor(
                    out=rows, in0=sums[chunk, n_tile][:],
                    scalar=neg_trans_b_col[:, n_tile : n_tile + 1], in1=rows,
                    op0=ALU.max, op1=ALU.add,
                )

        def transpose_out(chunk, r):
            out_rows = sbuf.tile([P, HIDDEN], F32, tag="out_rows", bufs=4)
            for g in range(PASSES):
                out_ps = psum.tile([P, BANK], F32, tag="out_ps")
                for t in range(PACK):
                    nc.tensor.transpose(
                        out_ps[:, t * P : (t + 1) * P],
                        h_T[chunk, g][:, t, r * P : (r + 1) * P],
                        ident_f32[:],
                    )
                if g == 0:
                    nc.scalar.copy(out=out_rows[:, g * BANK : (g + 1) * BANK], in_=out_ps[:])
                else:
                    nc.vector.tensor_copy(out=out_rows[:, g * BANK : (g + 1) * BANK], in_=out_ps[:])
            nc.sync.dma_start(out=out_chunks[chunk][:, r, :], in_=out_rows[:])

        def run(stage, step, lag):
            chunk, part = divmod(step - lag, PARTS)
            if 0 <= chunk < CHUNKS:
                stage(chunk, part)

        for step in range(CHUNKS * PARTS + LAG_OUT):
            if step % PARTS == 0 and step // PARTS + LOAD_AHEAD < CHUNKS:
                load_x(step // PARTS + LOAD_AHEAD)
            run(quantise, step, LAG_QUANTISE)
            run(finish, step, LAG_FINISH)
            run(transpose_out, step, LAG_OUT)
            run(transpose_x, step, 0)
            run(feature_layers, step, LAG_LAYER)
            run(mix, step, LAG_MIX)
            run(regroup, step, LAG_REGROUP)
            run(add_trans_b, step, LAG_BIAS)
